import numpy as np
import ml_dtypes

BF16 = ml_dtypes.bfloat16


def bf(x):
    return np.asarray(x, np.float32).astype(BF16)


def f32(x):
    return np.asarray(x, np.float32)


def f64(x):
    return np.asarray(x).astype(np.float64)


def striped(idx):
    return np.tile(idx.reshape(-1, 16).T, (8, 1))


T, NH, D, C, CO, S, L, NW, N = 3, 2, 128, 768, 256, 512, 256, 32, 8192
EPS = 1e-5
BASE = 10000.0


def pos_table():
    fr = D // 2
    inv = np.float32(1.0) / np.float32(BASE) ** (np.arange(fr, dtype=np.float32) / np.float32(fr))
    phase = np.arange(L, dtype=np.float32)[:, None] * inv
    return np.ascontiguousarray(np.concatenate([np.cos(f64(phase)), np.sin(f64(phase))], axis=-1).T)


def setup_inputs():
    return {"x": f32(np.random.standard_normal((C, S))), "pos": f32(pos_table()), "gamma": f32(1.0 + 0.1 * np.random.standard_normal((D, 1))), "beta": f32(0.1 * np.random.standard_normal((D, 1))), "offs": striped(np.concatenate([np.random.permutation(S)[:L] for _ in range(NW)]))}


def reference(x, pos, gamma, beta, offs):
    idx = offs[:16].T.reshape(-1)
    e = f64(x)[:, idx].reshape(T, NH, D, NW, L) + f64(pos)[:, None, :]
    outs = []
    for h in range(NH):
        q, k, v = e[0, h], e[1, h], e[2, h]
        sim = (q.transpose(1, 2, 0) @ k.transpose(1, 0, 2)) / np.sqrt(D)
        a = np.exp(sim - sim.max(axis=-1, keepdims=True))
        a = a / a.sum(axis=-1, keepdims=True)
        o = v.transpose(1, 0, 2) @ a.transpose(0, 2, 1)
        mu = o.mean(axis=1, keepdims=True)
        var = ((o - mu) ** 2).mean(axis=1, keepdims=True)
        y = (o - mu) / np.sqrt(var + EPS) * f64(gamma) + f64(beta)
        outs.append(y.transpose(1, 0, 2).reshape(D, N))
    return np.concatenate(outs, axis=0)

@@ -1,0 +1,144 @@
+import math
+
+import concourse.mybir as mybir
+from concourse.masks import make_identity
+
+F32 = mybir.dt.float32
+BF16 = mybir.dt.bfloat16
+U16 = mybir.dt.uint16
+ALU = mybir.AluOpType
+ACT = mybir.ActivationFunctionType
+AXIS = mybir.AxisListType
+
+P = 128
+HEADS = 2
+ALPHABET = 512
+PLACES = 256
+WORDS = 32
+HALVES = PLACES // P
+PAIR = 2 * PLACES
+EPS = 1e-5
+SUM_COL = math.sqrt(P * EPS)
+VC_STEP = 136
+VC_RING = 3
+
+FLOPS = 2 * 2 * P * PLACES * PLACES * HEADS * WORDS
+
+
+def tile_widthchartransformermlpheaderfastposv2_b_kernel(tc, x, pos, gamma, beta, offs, out):
+    nc = tc.nc
+    x_blocks = x.rearrange("(c p) s -> c p s", p=P)
+    out_by_head = out.rearrange("(h d) n -> d h n", h=HEADS)
+
+    with (
+        tc.tile_pool(name="held", bufs=1) as held,
+        tc.tile_pool(name="work", bufs=3) as work,
+        tc.psum_pool(name="psum", bufs=1) as psum,
+        nc.allow_low_precision(reason="the row maximum is only a shift of the softmax"),
+    ):
+        offsets = held.tile([P, WORDS * PLACES // 16], U16, name="offsets")
+        nc.sync.dma_start(offsets[:], offs)
+        pos2 = held.tile([P, PAIR], F32, name="pos2")
+        nc.scalar.dma_start(pos2[:, 0:PLACES], pos)
+        nc.gpsimd.dma_start(pos2[:, PLACES:PAIR], pos)
+        table = [held.tile([P, ALPHABET], F32, name="table%d" % c) for c in range(6)]
+        queues = [nc.sync, nc.scalar, nc.gpsimd]
+        for c in range(6):
+            queues[c % 3].dma_start(table[c][:], x_blocks[c])
+        gamma_in = held.tile([P, 1], F32, name="gamma_in")
+        nc.scalar.dma_start(gamma_in[:], gamma)
+        beta_in = held.tile([P, 1], F32, name="beta_in")
+        nc.gpsimd.dma_start(beta_in[:], beta)
+
+        ident32 = held.tile([P, P], F32, name="ident32")
+        make_identity(nc, ident32[:])
+        centre = held.tile([P, P], F32, name="centre")
+        nc.vector.tensor_scalar(out=centre[:], in0=ident32[:], scalar1=-1.0 / P, scalar2=None, op0=ALU.add)
+        ident = held.tile([P, P], BF16, name="ident")
+        make_identity(nc, ident[:])
+        minus_ident = held.tile([P, P], BF16, name="minus_ident")
+        nc.vector.tensor_scalar(out=minus_ident[:], in0=ident[:], scalar1=-1.0, scalar2=None, op0=ALU.mult)
+        minus_half = held.tile([P, HALVES], F32, name="minus_half")
+        nc.vector.memset(minus_half[:], -0.5)
+        gamma_scaled = held.tile([P, 1], F32, name="gamma_scaled")
+        nc.vector.tensor_scalar(out=gamma_scaled[:], in0=gamma_in[:], scalar1=math.sqrt(P), scalar2=None, op0=ALU.mult)
+        vc_ring = [held.tile([P, HEADS * HALVES, VC_STEP], BF16, name="vc%d" % k) for k in range(VC_RING)]
+        for vc in vc_ring:
+            nc.vector.memset(vc[:, :, P : P + 1], SUM_COL)
+
+        for pair in range(WORDS // 2):
+            pair_offsets = offsets[:, pair * (PAIR // 16) : (pair + 1) * (PAIR // 16)]
+            looked_up = []
+            for c in range(6):
+                e = work.tile([P, PAIR], F32, name="e%d" % c)
+                nc.vector.tensor_tensor(e[:], table[c][:].indirect(pair_offsets), pos2[:], ALU.add)
+                looked_up.append(e)
+            qk = []
+            for c in range(4):
+                rounded = work.tile([P, PAIR], BF16, name="qk%d" % c)
+                nc.gpsimd.tensor_scalar(out=rounded[:], in0=looked_up[c][:], scalar1=1.0, scalar2=0.0, op0=ALU.mult, op1=ALU.add)
+                qk.append(rounded)
+
+            for j in range(2):
+                word = 2 * pair + j
+                first = j * PLACES
+
+                vc_psum = psum.tile([P, HEADS * HALVES, P], F32, name="vc_psum")
+                for h in range(HEADS):
+                    for half in range(HALVES):
+                        r0 = first + half * P
+                        nc.tensor.matmul(vc_psum[:, h * HALVES + half, :], lhsT=looked_up[4 + h][:, r0 : r0 + P], rhs=centre[:], start=True, stop=True)
+                vc = vc_ring[word % VC_RING]
+                nc.scalar.copy(vc[:, :, 0:P], vc_psum[:])
+
+                normed_psum = psum.tile([P, HEADS, PLACES], F32, name="normed_psum")
+                for h in range(HEADS):
+                    q = qk[h]
+                    k = qk[2 + h]
+                    scores = psum.tile([P, HALVES, PLACES], F32, name="scores", bufs=2)
+                    for half in range(HALVES):
+                        i0 = first + half * P
+                        nc.tensor.matmul(scores[:, half, :], lhsT=q[:, i0 : i0 + P], rhs=k[:, first : first + PLACES], start=True, stop=True)
+                    top = work.tile([P, HALVES], BF16, name="top")
+                    nc.vector.tensor_reduce(out=top[:], in_=scores[:], axis=AXIS.X, op=ALU.max)
+
+                    scores_t = psum.tile([P, HALVES, PLACES], F32, name="scores_t", bufs=2)
+                    for rhalf in range(HALVES):
+                        r0 = first + rhalf * P
+                        nc.tensor.matmul(scores_t[:, rhalf, :], lhsT=k[:, r0 : r0 + P], rhs=q[:, first : first + PLACES], start=True, stop=False)
+                        for half in range(HALVES):
+                            nc.tensor.matmul(
+                                scores_t[:, rhalf, half * P : (half + 1) * P],
+                                lhsT=top[:, half : half + 1].to_broadcast([P, P]),
+                                rhs=minus_ident[:],
+                                start=False,
+                                stop=(half == HALVES - 1),
+                            )
+                    weights = work.tile([P, HALVES, PLACES], BF16, name="weights")
+                    nc.scalar.activation(out=weights[:], in_=scores_t[:], func=ACT.Exp, scale=1.0 / math.sqrt(P))
+
+                    o = psum.tile([P, HALVES, P + 1], F32, name="o", bufs=2)
+                    for half in range(HALVES):
+                        for rhalf in range(HALVES):
+                            nc.tensor.matmul(
+                                o[:, half, :],
+                                lhsT=weights[:, rhalf, half * P : (half + 1) * P],
+                                rhs=vc[:, h * HALVES + rhalf, 0 : P + 1],
+                                start=(rhalf == 0),
+                                stop=(rhalf == HALVES - 1),
+                            )
+
+                    square_sum = work.tile([P, HALVES], F32, name="square_sum")
+                    for half in range(HALVES):
+                        squares = work.tile([P, P + 1], BF16, name="squares")
+                        nc.scalar.activation(out=squares[:], in_=o[:, half, :], func=ACT.Square, accum_out=square_sum[:, half : half + 1])
+                    inv_norm = work.tile([P, HALVES], F32, name="inv_norm")
+                    nc.gpsimd.tensor_tensor(out=inv_norm[:], in0=square_sum[:], in1=minus_half[:], op=ALU.pow)
+                    normed = work.tile([P, HALVES, P], BF16, name="normed")
+                    for half in range(HALVES):
+                        nc.scalar.activation(out=normed[:, half, :], in_=o[:, half, 0:P], func=ACT.Copy, scale=inv_norm[:, half : half + 1])
+                        nc.tensor.matmul(normed_psum[:, h, half * P : (half + 1) * P], lhsT=normed[:, half, :], rhs=ident[:], start=True, stop=True)
+
+                result = work.tile([P, HEADS, PLACES], F32, name="result")
+                nc.scalar.activation(out=result[:], in_=normed_psum[:], func=ACT.Identity, scale=gamma_scaled[:, 0:1], bias=beta_in[:, 0:1])
+                nc.sync.dma_start(out_by_head[:, :, word * PLACES : (word + 1) * PLACES], result[:])

@@ -20,7 +20,8 @@ PAIR = 2 * PLACES
 EPS = 1e-5
 SUM_COL = math.sqrt(P * EPS)
 VC_STEP = 136
-VC_RING = 3
+VC_RING = 4
+GROUPS = HEADS * WORDS // 2
 
 FLOPS = 2 * 2 * P * PLACES * PLACES * HEADS * WORDS
 
@@ -28,7 +29,6 @@ FLOPS = 2 * 2 * P * PLACES * PLACES * HEADS * WORDS
 def tile_widthchartransformermlpheaderfastposv2_b_kernel(tc, x, pos, gamma, beta, offs, out):
     nc = tc.nc
     x_blocks = x.rearrange("(c p) s -> c p s", p=P)
-    out_by_head = out.rearrange("(h d) n -> d h n", h=HEADS)
 
     with (
         tc.tile_pool(name="held", bufs=1) as held,
@@ -40,15 +40,15 @@ def tile_widthchartransformermlpheaderfastposv2_b_kernel(tc, x, pos, gamma, beta
         nc.sync.dma_start(offsets[:], offs)
         pos2 = held.tile([P, PAIR], F32, name="pos2")
         nc.scalar.dma_start(pos2[:, 0:PLACES], pos)
-        nc.gpsimd.dma_start(pos2[:, PLACES:PAIR], pos)
+        nc.scalar.dma_start(pos2[:, PLACES:PAIR], pos)
         table = [held.tile([P, ALPHABET], F32, name="table%d" % c) for c in range(6)]
-        queues = [nc.sync, nc.scalar, nc.gpsimd]
-        for c in range(6):
-            queues[c % 3].dma_start(table[c][:], x_blocks[c])
+        for c in (0, 2, 4, 1, 3, 5):
+            queue = nc.sync if c < 3 else nc.scalar
+            queue.dma_start(table[c][:], x_blocks[c])
         gamma_in = held.tile([P, 1], F32, name="gamma_in")
-        nc.scalar.dma_start(gamma_in[:], gamma)
+        nc.sync.dma_start(gamma_in[:], gamma)
         beta_in = held.tile([P, 1], F32, name="beta_in")
-        nc.gpsimd.dma_start(beta_in[:], beta)
+        nc.scalar.dma_start(beta_in[:], beta)
 
         ident32 = held.tile([P, P], F32, name="ident32")
         make_identity(nc, ident32[:])
@@ -58,87 +58,104 @@ def tile_widthchartransformermlpheaderfastposv2_b_kernel(tc, x, pos, gamma, beta
         make_identity(nc, ident[:])
         minus_ident = held.tile([P, P], BF16, name="minus_ident")
         nc.vector.tensor_scalar(out=minus_ident[:], in0=ident[:], scalar1=-1.0, scalar2=None, op0=ALU.mult)
-        minus_half = held.tile([P, HALVES], F32, name="minus_half")
+        minus_half = held.tile([P, 2 * HALVES], F32, name="minus_half")
         nc.vector.memset(minus_half[:], -0.5)
         gamma_scaled = held.tile([P, 1], F32, name="gamma_scaled")
         nc.vector.tensor_scalar(out=gamma_scaled[:], in0=gamma_in[:], scalar1=math.sqrt(P), scalar2=None, op0=ALU.mult)
-        vc_ring = [held.tile([P, HEADS * HALVES, VC_STEP], BF16, name="vc%d" % k) for k in range(VC_RING)]
+        vc_ring = [held.tile([P, 2 * HALVES, VC_STEP], BF16, name="vc%d" % n) for n in range(VC_RING)]
         for vc in vc_ring:
             nc.vector.memset(vc[:, :, P : P + 1], SUM_COL)
 
-        for pair in range(WORDS // 2):
+        q16, k16, v32, tops, weights, contexts, inv_norms = {}, {}, {}, {}, {}, {}, {}
+
+        def look_up(g):
+            pair, h = divmod(g, HEADS)
             pair_offsets = offsets[:, pair * (PAIR // 16) : (pair + 1) * (PAIR // 16)]
-            looked_up = []
-            for c in range(6):
-                e = work.tile([P, PAIR], F32, name="e%d" % c)
-                nc.vector.tensor_tensor(e[:], table[c][:].indirect(pair_offsets), pos2[:], ALU.add)
-                looked_up.append(e)
-            qk = []
-            for c in range(4):
-                rounded = work.tile([P, PAIR], BF16, name="qk%d" % c)
-                nc.gpsimd.tensor_scalar(out=rounded[:], in0=looked_up[c][:], scalar1=1.0, scalar2=0.0, op0=ALU.mult, op1=ALU.add)
-                qk.append(rounded)
+            q32 = work.tile([P, PAIR], F32, name="q32")
+            nc.vector.tensor_tensor(q32[:], table[h][:].indirect(pair_offsets), pos2[:], ALU.add)
+            k32 = work.tile([P, PAIR], F32, name="k32")
+            nc.vector.tensor_tensor(k32[:], table[2 + h][:].indirect(pair_offsets), pos2[:], ALU.add)
+            q16[g] = work.tile([P, PAIR], BF16, name="q16", bufs=4)
+            nc.vector.tensor_copy(out=q16[g][:], in_=q32[:])
+            k16[g] = work.tile([P, PAIR], BF16, name="k16", bufs=4)
+            nc.scalar.copy(k16[g][:], k32[:])
+            v32[g] = work.tile([P, PAIR], F32, name="v32")
+            nc.vector.tensor_tensor(v32[g][:], table[4 + h][:].indirect(pair_offsets), pos2[:], ALU.add)
 
+        def centre_values(g):
+            vc_psum = psum.tile([P, 2 * HALVES, P], F32, name="vc_psum")
+            for block in range(2 * HALVES):
+                nc.tensor.matmul(vc_psum[:, block, :], lhsT=v32[g][:, block * P : (block + 1) * P], rhs=centre[:], start=True, stop=True)
+            nc.scalar.copy(vc_ring[g % VC_RING][:, :, 0:P], vc_psum[:])
+
+        def row_maxima(g):
+            tops[g] = work.tile([P, 2, HALVES], BF16, name="top", bufs=4)
             for j in range(2):
-                word = 2 * pair + j
                 first = j * PLACES
+                scores = psum.tile([P, HALVES, PLACES], F32, name="scores", bufs=2)
+                for half in range(HALVES):
+                    i0 = first + half * P
+                    nc.tensor.matmul(scores[:, half, :], lhsT=q16[g][:, i0 : i0 + P], rhs=k16[g][:, first : first + PLACES], start=True, stop=True)
+                nc.vector.tensor_reduce(out=tops[g][:, j, :], in_=scores[:], axis=AXIS.X, op=ALU.max)
 
-                vc_psum = psum.tile([P, HEADS * HALVES, P], F32, name="vc_psum")
-                for h in range(HEADS):
+        def attention_weights(g):
+            weights[g] = []
+            for j in range(2):
+                first = j * PLACES
+                scores_t = psum.tile([P, HALVES, PLACES], F32, name="scores_t", bufs=2)
+                for rhalf in range(HALVES):
+                    r0 = first + rhalf * P
+                    nc.tensor.matmul(scores_t[:, rhalf, :], lhsT=k16[g][:, r0 : r0 + P], rhs=q16[g][:, first : first + PLACES], start=True, stop=False)
                     for half in range(HALVES):
-                        r0 = first + half * P
-                        nc.tensor.matmul(vc_psum[:, h * HALVES + half, :], lhsT=looked_up[4 + h][:, r0 : r0 + P], rhs=centre[:], start=True, stop=True)
-                vc = vc_ring[word % VC_RING]
-                nc.scalar.copy(vc[:, :, 0:P], vc_psum[:])
+                        nc.tensor.matmul(
+                            scores_t[:, rhalf, half * P : (half + 1) * P],
+                            lhsT=tops[g][:, j, half : half + 1].to_broadcast([P, P]),
+                            rhs=minus_ident[:],
+                            start=False,
+                            stop=(half == HALVES - 1),
+                        )
+                w16 = work.tile([P, HALVES, PLACES], BF16, name="w16", bufs=6)
+                nc.scalar.activation(out=w16[:], in_=scores_t[:], func=ACT.Exp, scale=1.0 / math.sqrt(P))
+                weights[g].append(w16)
 
-                normed_psum = psum.tile([P, HEADS, PLACES], F32, name="normed_psum")
-                for h in range(HEADS):
-                    q = qk[h]
-                    k = qk[2 + h]
-                    scores = psum.tile([P, HALVES, PLACES], F32, name="scores", bufs=2)
-                    for half in range(HALVES):
-                        i0 = first + half * P
-                        nc.tensor.matmul(scores[:, half, :], lhsT=q[:, i0 : i0 + P], rhs=k[:, first : first + PLACES], start=True, stop=True)
-                    top = work.tile([P, HALVES], BF16, name="top")
-                    nc.vector.tensor_reduce(out=top[:], in_=scores[:], axis=AXIS.X, op=ALU.max)
-
-                    scores_t = psum.tile([P, HALVES, PLACES], F32, name="scores_t", bufs=2)
+        def context(g):
+            vc = vc_ring[g % VC_RING]
+            contexts[g] = []
+            square_sum = work.tile([P, 2 * HALVES], F32, name="square_sum")
+            for j in range(2):
+                o = psum.tile([P, HALVES, P + 1], F32, name="o", bufs=2)
+                for half in range(HALVES):
                     for rhalf in range(HALVES):
-                        r0 = first + rhalf * P
-                        nc.tensor.matmul(scores_t[:, rhalf, :], lhsT=k[:, r0 : r0 + P], rhs=q[:, first : first + PLACES], start=True, stop=False)
-                        for half in range(HALVES):
-                            nc.tensor.matmul(
-                                scores_t[:, rhalf, half * P : (half + 1) * P],
-                                lhsT=top[:, half : half + 1].to_broadcast([P, P]),
-                                rhs=minus_ident[:],
-                                start=False,
-                                stop=(half == HALVES - 1),
-                            )
-                    weights = work.tile([P, HALVES, PLACES], BF16, name="weights")
-                    nc.scalar.activation(out=weights[:], in_=scores_t[:], func=ACT.Exp, scale=1.0 / math.sqrt(P))
+                        nc.tensor.matmul(
+                            o[:, half, :],
+                            lhsT=weights[g][j][:, rhalf, half * P : (half + 1) * P],
+                            rhs=vc[:, j * HALVES + rhalf, 0 : P + 1],
+                            start=(rhalf == 0),
+                            stop=(rhalf == HALVES - 1),
+                        )
+                for half in range(HALVES):
+                    squares = work.tile([P, P + 1], BF16, name="squares")
+                    column = j * HALVES + half
+                    nc.scalar.activation(out=squares[:], in_=o[:, half, :], func=ACT.Square, accum_out=square_sum[:, column : column + 1])
+                contexts[g].append(o)
+            inv_norms[g] = work.tile([P, 2 * HALVES], F32, name="inv_norm")
+            nc.gpsimd.tensor_tensor(out=inv_norms[g][:], in0=square_sum[:], in1=minus_half[:], op=ALU.pow)
 
-                    o = psum.tile([P, HALVES, P + 1], F32, name="o", bufs=2)
-                    for half in range(HALVES):
-                        for rhalf in range(HALVES):
-                            nc.tensor.matmul(
-                                o[:, half, :],
-                                lhsT=weights[:, rhalf, half * P : (half + 1) * P],
-                                rhs=vc[:, h * HALVES + rhalf, 0 : P + 1],
-                                start=(rhalf == 0),
-                                stop=(rhalf == HALVES - 1),
-                            )
+        def normalise(g):
+            pair, h = divmod(g, HEADS)
+            normed_psum = psum.tile([P, PAIR], F32, name="normed_psum")
+            for j in range(2):
+                for half in range(HALVES):
+                    column = j * HALVES + half
+                    normed = work.tile([P, P], BF16, name="normed", bufs=4)
+                    nc.scalar.activation(out=normed[:], in_=contexts[g][j][:, half, 0:P], func=ACT.Copy, scale=inv_norms[g][:, column : column + 1])
+                    nc.tensor.matmul(normed_psum[:, column * P : (column + 1) * P], lhsT=normed[:], rhs=ident[:], start=True, stop=True)
+            result = work.tile([P, PAIR], F32, name="result")
+            nc.scalar.activation(out=result[:], in_=normed_psum[:], func=ACT.Identity, scale=gamma_scaled[:, 0:1], bias=beta_in[:, 0:1])
+            nc.sync.dma_start(out[h * P : (h + 1) * P, pair * PAIR : (pair + 1) * PAIR], result[:])
 
-                    square_sum = work.tile([P, HALVES], F32, name="square_sum")
-                    for half in range(HALVES):
-                        squares = work.tile([P, P + 1], BF16, name="squares")
-                        nc.scalar.activation(out=squares[:], in_=o[:, half, :], func=ACT.Square, accum_out=square_sum[:, half : half + 1])
-                    inv_norm = work.tile([P, HALVES], F32, name="inv_norm")
-                    nc.gpsimd.tensor_tensor(out=inv_norm[:], in0=square_sum[:], in1=minus_half[:], op=ALU.pow)
-                    normed = work.tile([P, HALVES, P], BF16, name="normed")
-                    for half in range(HALVES):
-                        nc.scalar.activation(out=normed[:, half, :], in_=o[:, half, 0:P], func=ACT.Copy, scale=inv_norm[:, half : half + 1])
-                        nc.tensor.matmul(normed_psum[:, h, half * P : (half + 1) * P], lhsT=normed[:, half, :], rhs=ident[:], start=True, stop=True)
-
-                result = work.tile([P, HEADS, PLACES], F32, name="result")
-                nc.scalar.activation(out=result[:], in_=normed_psum[:], func=ACT.Identity, scale=gamma_scaled[:, 0:1], bias=beta_in[:, 0:1])
-                nc.sync.dma_start(out_by_head[:, :, word * PLACES : (word + 1) * PLACES], result[:])
+        stages = [(normalise, 4), (context, 3), (attention_weights, 2), (look_up, 0), (centre_values, 1), (row_maxima, 1)]
+        for step in range(GROUPS + 4):
+            for stage, lag in stages:
+                if 0 <= step - lag < GROUPS:
+                    stage(step - lag)

@@ -17,11 +17,23 @@ PLACES = 256
 WORDS = 32
 HALVES = PLACES // P
 PAIR = 2 * PLACES
+BLOCKS = PAIR // P
+GROUPS = HEADS * WORDS // 2
 EPS = 1e-5
 SUM_COL = math.sqrt(P * EPS)
 VC_STEP = 136
-VC_RING = 4
-GROUPS = HEADS * WORDS // 2
+
+SCORE = 1
+MAXIMA = 2
+VALUES = 2
+WEIGHTS = 3
+CONTEXT = 4
+NORMALISE = 5
+
+
+def alive(written, last_read):
+    return last_read - written + 1
+
 
 FLOPS = 2 * 2 * P * PLACES * PLACES * HEADS * WORDS
 
@@ -32,7 +44,7 @@ def tile_widthchartransformermlpheaderfastposv2_b_kernel(tc, x, pos, gamma, beta
 
     with (
         tc.tile_pool(name="held", bufs=1) as held,
-        tc.tile_pool(name="work", bufs=3) as work,
+        tc.tile_pool(name="work", bufs=2) as work,
         tc.psum_pool(name="psum", bufs=1) as psum,
         nc.allow_low_precision(reason="the row maximum is only a shift of the softmax"),
     ):
@@ -58,15 +70,15 @@ def tile_widthchartransformermlpheaderfastposv2_b_kernel(tc, x, pos, gamma, beta
         make_identity(nc, ident[:])
         minus_ident = held.tile([P, P], BF16, name="minus_ident")
         nc.vector.tensor_scalar(out=minus_ident[:], in0=ident[:], scalar1=-1.0, scalar2=None, op0=ALU.mult)
-        minus_half = held.tile([P, 2 * HALVES], F32, name="minus_half")
+        minus_half = held.tile([P, BLOCKS], F32, name="minus_half")
         nc.vector.memset(minus_half[:], -0.5)
         gamma_scaled = held.tile([P, 1], F32, name="gamma_scaled")
         nc.vector.tensor_scalar(out=gamma_scaled[:], in0=gamma_in[:], scalar1=math.sqrt(P), scalar2=None, op0=ALU.mult)
-        vc_ring = [held.tile([P, 2 * HALVES, VC_STEP], BF16, name="vc%d" % n) for n in range(VC_RING)]
+        vc_ring = [held.tile([P, BLOCKS, VC_STEP], BF16, name="vc%d" % n) for n in range(alive(VALUES, CONTEXT))]
         for vc in vc_ring:
             nc.vector.memset(vc[:, :, P : P + 1], SUM_COL)
 
-        q16, k16, v32, tops, weights, contexts, inv_norms = {}, {}, {}, {}, {}, {}, {}
+        q16, k16, v32, scores, tops, weights, contexts, inv_norms, normeds = {}, {}, {}, {}, {}, {}, {}, {}, {}
 
         def look_up(g):
             pair, h = divmod(g, HEADS)
@@ -75,87 +87,98 @@ def tile_widthchartransformermlpheaderfastposv2_b_kernel(tc, x, pos, gamma, beta
             nc.vector.tensor_tensor(q32[:], table[h][:].indirect(pair_offsets), pos2[:], ALU.add)
             k32 = work.tile([P, PAIR], F32, name="k32")
             nc.vector.tensor_tensor(k32[:], table[2 + h][:].indirect(pair_offsets), pos2[:], ALU.add)
-            q16[g] = work.tile([P, PAIR], BF16, name="q16", bufs=4)
+            q16[g] = work.tile([P, PAIR], BF16, name="q16", bufs=alive(0, WEIGHTS))
             nc.vector.tensor_copy(out=q16[g][:], in_=q32[:])
-            k16[g] = work.tile([P, PAIR], BF16, name="k16", bufs=4)
+            k16[g] = work.tile([P, PAIR], BF16, name="k16", bufs=alive(0, WEIGHTS))
             nc.scalar.copy(k16[g][:], k32[:])
-            v32[g] = work.tile([P, PAIR], F32, name="v32")
+            v32[g] = work.tile([P, PAIR], F32, name="v32", bufs=alive(0, VALUES))
             nc.vector.tensor_tensor(v32[g][:], table[4 + h][:].indirect(pair_offsets), pos2[:], ALU.add)
 
-        def centre_values(g):
-            vc_psum = psum.tile([P, 2 * HALVES, P], F32, name="vc_psum")
-            for block in range(2 * HALVES):
-                nc.tensor.matmul(vc_psum[:, block, :], lhsT=v32[g][:, block * P : (block + 1) * P], rhs=centre[:], start=True, stop=True)
-            nc.scalar.copy(vc_ring[g % VC_RING][:, :, 0:P], vc_psum[:])
+        def score(g):
+            scores[g] = psum.tile([P, BLOCKS, PLACES], BF16, name="scores", bufs=alive(SCORE, MAXIMA))
+            for block in range(BLOCKS):
+                first = (block // HALVES) * PLACES
+                nc.tensor.matmul(scores[g][:, block, :], lhsT=q16[g][:, block * P : (block + 1) * P], rhs=k16[g][:, first : first + PLACES], start=True, stop=True)
 
         def row_maxima(g):
-            tops[g] = work.tile([P, 2, HALVES], BF16, name="top", bufs=4)
-            for j in range(2):
-                first = j * PLACES
-                scores = psum.tile([P, HALVES, PLACES], F32, name="scores", bufs=2)
-                for half in range(HALVES):
-                    i0 = first + half * P
-                    nc.tensor.matmul(scores[:, half, :], lhsT=q16[g][:, i0 : i0 + P], rhs=k16[g][:, first : first + PLACES], start=True, stop=True)
-                nc.vector.tensor_reduce(out=tops[g][:, j, :], in_=scores[:], axis=AXIS.X, op=ALU.max)
+            tops[g] = work.tile([P, BLOCKS], BF16, name="top", bufs=alive(MAXIMA, WEIGHTS))
+            nc.vector.tensor_reduce(out=tops[g][:], in_=scores[g][:], axis=AXIS.X, op=ALU.max)
+
+        def centre_values(g):
+            vc_psum = psum.tile([P, BLOCKS, P], F32, name="vc_psum")
+            for block in range(BLOCKS):
+                nc.tensor.matmul(vc_psum[:, block, :], lhsT=v32[g][:, block * P : (block + 1) * P], rhs=centre[:], start=True, stop=True)
+            nc.scalar.copy(vc_ring[g % len(vc_ring)][:, :, 0:P], vc_psum[:])
 
         def attention_weights(g):
             weights[g] = []
-            for j in range(2):
-                first = j * PLACES
+            for word in range(2):
+                first = word * PLACES
                 scores_t = psum.tile([P, HALVES, PLACES], F32, name="scores_t", bufs=2)
                 for rhalf in range(HALVES):
                     r0 = first + rhalf * P
                     nc.tensor.matmul(scores_t[:, rhalf, :], lhsT=k16[g][:, r0 : r0 + P], rhs=q16[g][:, first : first + PLACES], start=True, stop=False)
                     for half in range(HALVES):
+                        block = word * HALVES + half
                         nc.tensor.matmul(
                             scores_t[:, rhalf, half * P : (half + 1) * P],
-                            lhsT=tops[g][:, j, half : half + 1].to_broadcast([P, P]),
+                            lhsT=tops[g][:, block : block + 1].to_broadcast([P, P]),
                             rhs=minus_ident[:],
                             start=False,
                             stop=(half == HALVES - 1),
                         )
-                w16 = work.tile([P, HALVES, PLACES], BF16, name="w16", bufs=6)
+                w16 = work.tile([P, HALVES, PLACES], BF16, name="w16", bufs=2 * alive(WEIGHTS, CONTEXT))
                 nc.scalar.activation(out=w16[:], in_=scores_t[:], func=ACT.Exp, scale=1.0 / math.sqrt(P))
                 weights[g].append(w16)
 
         def context(g):
-            vc = vc_ring[g % VC_RING]
+            vc = vc_ring[g % len(vc_ring)]
             contexts[g] = []
-            square_sum = work.tile([P, 2 * HALVES], F32, name="square_sum")
-            for j in range(2):
+            square_sum = work.tile([P, BLOCKS], F32, name="square_sum")
+            for word in range(2):
                 o = psum.tile([P, HALVES, P + 1], F32, name="o", bufs=2)
                 for half in range(HALVES):
                     for rhalf in range(HALVES):
                         nc.tensor.matmul(
                             o[:, half, :],
-                            lhsT=weights[g][j][:, rhalf, half * P : (half + 1) * P],
-                            rhs=vc[:, j * HALVES + rhalf, 0 : P + 1],
+                            lhsT=weights[g][word][:, rhalf, half * P : (half + 1) * P],
+                            rhs=vc[:, word * HALVES + rhalf, 0 : P + 1],
                             start=(rhalf == 0),
                             stop=(rhalf == HALVES - 1),
                         )
                 for half in range(HALVES):
+                    block = word * HALVES + half
                     squares = work.tile([P, P + 1], BF16, name="squares")
-                    column = j * HALVES + half
-                    nc.scalar.activation(out=squares[:], in_=o[:, half, :], func=ACT.Square, accum_out=square_sum[:, column : column + 1])
+                    nc.scalar.activation(out=squares[:], in_=o[:, half, :], func=ACT.Square, accum_out=square_sum[:, block : block + 1])
                 contexts[g].append(o)
-            inv_norms[g] = work.tile([P, 2 * HALVES], F32, name="inv_norm")
+            inv_norms[g] = work.tile([P, BLOCKS], F32, name="inv_norm", bufs=alive(CONTEXT, NORMALISE))
             nc.gpsimd.tensor_tensor(out=inv_norms[g][:], in0=square_sum[:], in1=minus_half[:], op=ALU.pow)
 
         def normalise(g):
+            normeds[g] = work.tile([P, BLOCKS, P], BF16, name="normed")
+            for block in range(BLOCKS):
+                word, half = divmod(block, HALVES)
+                nc.scalar.activation(out=normeds[g][:, block, :], in_=contexts[g][word][:, half, 0:P], func=ACT.Copy, scale=inv_norms[g][:, block : block + 1])
+
+        def store(g):
             pair, h = divmod(g, HEADS)
             normed_psum = psum.tile([P, PAIR], F32, name="normed_psum")
-            for j in range(2):
-                for half in range(HALVES):
-                    column = j * HALVES + half
-                    normed = work.tile([P, P], BF16, name="normed", bufs=4)
-                    nc.scalar.activation(out=normed[:], in_=contexts[g][j][:, half, 0:P], func=ACT.Copy, scale=inv_norms[g][:, column : column + 1])
-                    nc.tensor.matmul(normed_psum[:, column * P : (column + 1) * P], lhsT=normed[:], rhs=ident[:], start=True, stop=True)
+            for block in range(BLOCKS):
+                nc.tensor.matmul(normed_psum[:, block * P : (block + 1) * P], lhsT=normeds[g][:, block, :], rhs=ident[:], start=True, stop=True)
             result = work.tile([P, PAIR], F32, name="result")
             nc.scalar.activation(out=result[:], in_=normed_psum[:], func=ACT.Identity, scale=gamma_scaled[:, 0:1], bias=beta_in[:, 0:1])
             nc.sync.dma_start(out[h * P : (h + 1) * P, pair * PAIR : (pair + 1) * PAIR], result[:])
 
-        stages = [(normalise, 4), (context, 3), (attention_weights, 2), (look_up, 0), (centre_values, 1), (row_maxima, 1)]
-        for step in range(GROUPS + 4):
-            for stage, lag in stages:
-                if 0 <= step - lag < GROUPS:
-                    stage(step - lag)
+        def run(stage, g):
+            if 0 <= g < GROUPS:
+                stage(g)
+
+        for step in range(GROUPS + NORMALISE):
+            run(normalise, step - NORMALISE)
+            run(context, step - CONTEXT)
+            run(attention_weights, step - WEIGHTS)
+            run(store, step - NORMALISE)
+            run(centre_values, step - VALUES)
+            run(score, step - SCORE)
+            run(look_up, step)
+            run(row_maxima, step - MAXIMA)

@@ -148,7 +148,7 @@ def tile_widthchartransformermlpheaderfastposv2_b_kernel(tc, x, pos, gamma, beta
                         )
                 for half in range(HALVES):
                     block = word * HALVES + half
-                    squares = work.tile([P, P + 1], BF16, name="squares")
+                    squares = work.tile([P, P + 1], BF16, name="squares", bufs=BLOCKS)
                     nc.scalar.activation(out=squares[:], in_=o[:, half, :], func=ACT.Square, accum_out=square_sum[:, block : block + 1])
                 contexts[g].append(o)
             inv_norms[g] = work.tile([P, BLOCKS], F32, name="inv_norm", bufs=alive(CONTEXT, NORMALISE))

@@ -25,10 +25,10 @@ VC_STEP = 136
 
 SCORE = 1
 MAXIMA = 2
-VALUES = 2
 WEIGHTS = 3
 CONTEXT = 4
 NORMALISE = 5
+VALUES = CONTEXT // 2
 
 
 def alive(written, last_read):
@@ -88,7 +88,7 @@ def tile_widthchartransformermlpheaderfastposv2_b_kernel(tc, x, pos, gamma, beta
             k32 = work.tile([P, PAIR], F32, name="k32")
             nc.vector.tensor_tensor(k32[:], table[2 + h][:].indirect(pair_offsets), pos2[:], ALU.add)
             q16[g] = work.tile([P, PAIR], BF16, name="q16", bufs=alive(0, WEIGHTS))
-            nc.vector.tensor_copy(out=q16[g][:], in_=q32[:])
+            nc.scalar.copy(q16[g][:], q32[:])
             k16[g] = work.tile([P, PAIR], BF16, name="k16", bufs=alive(0, WEIGHTS))
             nc.scalar.copy(k16[g][:], k32[:])
             v32[g] = work.tile([P, PAIR], F32, name="v32", bufs=alive(0, VALUES))

@@ -52,7 +52,6 @@ def tile_widthchartransformermlpheaderfastposv2_b_kernel(tc, x, pos, gamma, beta
         nc.sync.dma_start(offsets[:], offs)
         pos2 = held.tile([P, PAIR], F32, name="pos2")
         nc.scalar.dma_start(pos2[:, 0:PLACES], pos)
-        nc.scalar.dma_start(pos2[:, PLACES:PAIR], pos)
         table = [held.tile([P, ALPHABET], F32, name="table%d" % c) for c in range(6)]
         for c in (0, 2, 4, 1, 3, 5):
             queue = nc.sync if c < 3 else nc.scalar
@@ -61,6 +60,8 @@ def tile_widthchartransformermlpheaderfastposv2_b_kernel(tc, x, pos, gamma, beta
         nc.sync.dma_start(gamma_in[:], gamma)
         beta_in = held.tile([P, 1], F32, name="beta_in")
         nc.scalar.dma_start(beta_in[:], beta)
+
+        nc.vector.tensor_copy(pos2[:, PLACES:PAIR], pos2[:, 0:PLACES])
 
         ident32 = held.tile([P, P], F32, name="ident32")
         make_identity(nc, ident32[:])
@@ -80,17 +81,18 @@ def tile_widthchartransformermlpheaderfastposv2_b_kernel(tc, x, pos, gamma, beta
 
         q16, k16, v32, scores, tops, weights, contexts, inv_norms, normeds = {}, {}, {}, {}, {}, {}, {}, {}, {}
 
+        def upper_halves(tile32):
+            return tile32[:].bitcast(BF16).rearrange("p (n two) -> p n two", two=2)
+
         def look_up(g):
             pair, h = divmod(g, HEADS)
             pair_offsets = offsets[:, pair * (PAIR // 16) : (pair + 1) * (PAIR // 16)]
-            q32 = work.tile([P, PAIR], F32, name="q32")
+            q32 = work.tile([P, PAIR], F32, name="q32", bufs=alive(0, WEIGHTS))
             nc.vector.tensor_tensor(q32[:], table[h][:].indirect(pair_offsets), pos2[:], ALU.add)
-            k32 = work.tile([P, PAIR], F32, name="k32")
+            k32 = work.tile([P, PAIR], F32, name="k32", bufs=alive(0, WEIGHTS))
             nc.vector.tensor_tensor(k32[:], table[2 + h][:].indirect(pair_offsets), pos2[:], ALU.add)
-            q16[g] = work.tile([P, PAIR], BF16, name="q16", bufs=alive(0, WEIGHTS))
-            nc.scalar.copy(q16[g][:], q32[:])
-            k16[g] = work.tile([P, PAIR], BF16, name="k16", bufs=alive(0, WEIGHTS))
-            nc.scalar.copy(k16[g][:], k32[:])
+            q16[g] = upper_halves(q32)
+            k16[g] = upper_halves(k32)
             v32[g] = work.tile([P, PAIR], F32, name="v32", bufs=alive(0, VALUES))
             nc.vector.tensor_tensor(v32[g][:], table[4 + h][:].indirect(pair_offsets), pos2[:], ALU.add)
 
@@ -98,7 +100,7 @@ def tile_widthchartransformermlpheaderfastposv2_b_kernel(tc, x, pos, gamma, beta
             scores[g] = psum.tile([P, BLOCKS, PLACES], BF16, name="scores", bufs=alive(SCORE, MAXIMA))
             for block in range(BLOCKS):
                 first = (block // HALVES) * PLACES
-                nc.tensor.matmul(scores[g][:, block, :], lhsT=q16[g][:, block * P : (block + 1) * P], rhs=k16[g][:, first : first + PLACES], start=True, stop=True)
+                nc.tensor.matmul(scores[g][:, block, :], lhsT=q16[g][:, block * P : (block + 1) * P, 1], rhs=k16[g][:, first : first + PLACES, 1], start=True, stop=True)
 
         def row_maxima(g):
             tops[g] = work.tile([P, BLOCKS], BF16, name="top", bufs=alive(MAXIMA, WEIGHTS))
@@ -117,7 +119,7 @@ def tile_widthchartransformermlpheaderfastposv2_b_kernel(tc, x, pos, gamma, beta
                 scores_t = psum.tile([P, HALVES, PLACES], F32, name="scores_t", bufs=2)
                 for rhalf in range(HALVES):
                     r0 = first + rhalf * P
-                    nc.tensor.matmul(scores_t[:, rhalf, :], lhsT=k16[g][:, r0 : r0 + P], rhs=q16[g][:, first : first + PLACES], start=True, stop=False)
+                    nc.tensor.matmul(scores_t[:, rhalf, :], lhsT=k16[g][:, r0 : r0 + P, 1], rhs=q16[g][:, first : first + PLACES, 1], start=True, stop=False)
                     for half in range(HALVES):
                         block = word * HALVES + half
                         nc.tensor.matmul(

@@ -6,6 +6,7 @@ from concourse.masks import make_identity
 F32 = mybir.dt.float32
 BF16 = mybir.dt.bfloat16
 U16 = mybir.dt.uint16
+U32 = mybir.dt.uint32
 ALU = mybir.AluOpType
 ACT = mybir.ActivationFunctionType
 AXIS = mybir.AxisListType
@@ -22,6 +23,21 @@ GROUPS = HEADS * WORDS // 2
 EPS = 1e-5
 SUM_COL = math.sqrt(P * EPS)
 VC_STEP = 136
+
+LN2 = math.log(2.0)
+M_PEAK = 1.0 / LN2 - 1.0
+LOG_GAP = (math.log(1.0 + M_PEAK) / LN2 - M_PEAK) / 2.0
+LOG_STEP = -(LN2 / 2.0) / 2.0**23
+LOG_BASE = (LN2 / 2.0) * (127.0 - LOG_GAP)
+
+FIT_HALF = 0.1
+FIT_POINTS = [1.0 + FIT_HALF * math.cos((2 * n + 1) * math.pi / 6.0) for n in range(3)]
+FIT_VALUES = [-0.5 * math.log(t) for t in FIT_POINTS]
+SLOPE_01 = (FIT_VALUES[1] - FIT_VALUES[0]) / (FIT_POINTS[1] - FIT_POINTS[0])
+SLOPE_12 = (FIT_VALUES[2] - FIT_VALUES[1]) / (FIT_POINTS[2] - FIT_POINTS[1])
+FIT_A = (SLOPE_12 - SLOPE_01) / (FIT_POINTS[2] - FIT_POINTS[0])
+FIT_T = (FIT_POINTS[0] + FIT_POINTS[1]) / 2.0 - SLOPE_01 / (2.0 * FIT_A)
+FIT_C = FIT_VALUES[0] - FIT_A * (FIT_POINTS[0] - FIT_T) ** 2
 
 SCORE = 1
 MAXIMA = 2
@@ -71,8 +87,12 @@ def tile_widthchartransformermlpheaderfastposv2_b_kernel(tc, x, pos, gamma, beta
         make_identity(nc, ident[:])
         minus_ident = held.tile([P, P], BF16, name="minus_ident")
         nc.vector.tensor_scalar(out=minus_ident[:], in0=ident[:], scalar1=-1.0, scalar2=None, op0=ALU.mult)
-        minus_half = held.tile([P, BLOCKS], F32, name="minus_half")
-        nc.vector.memset(minus_half[:], -0.5)
+        bias_guess_sq = held.tile([P, 1], F32, name="bias_guess_sq")
+        nc.vector.memset(bias_guess_sq[:], 2.0 * LOG_BASE)
+        bias_log_guess = held.tile([P, 1], F32, name="bias_log_guess")
+        nc.vector.memset(bias_log_guess[:], LOG_BASE + FIT_C)
+        bias_fit = held.tile([P, 1], F32, name="bias_fit")
+        nc.vector.memset(bias_fit[:], -FIT_T)
         gamma_scaled = held.tile([P, 1], F32, name="gamma_scaled")
         nc.vector.tensor_scalar(out=gamma_scaled[:], in0=gamma_in[:], scalar1=math.sqrt(P), scalar2=None, op0=ALU.mult)
         vc_ring = [held.tile([P, BLOCKS, VC_STEP], BF16, name="vc%d" % n) for n in range(alive(VALUES, CONTEXT))]
@@ -136,7 +156,7 @@ def tile_widthchartransformermlpheaderfastposv2_b_kernel(tc, x, pos, gamma, beta
         def context(g):
             vc = vc_ring[g % len(vc_ring)]
             contexts[g] = []
-            square_sum = work.tile([P, BLOCKS], F32, name="square_sum")
+            inv_norms[g] = work.tile([P, BLOCKS], F32, name="inv_norm", bufs=alive(CONTEXT, NORMALISE))
             for word in range(2):
                 o = psum.tile([P, HALVES, P + 1], F32, name="o", bufs=2)
                 for half in range(HALVES):
@@ -148,13 +168,23 @@ def tile_widthchartransformermlpheaderfastposv2_b_kernel(tc, x, pos, gamma, beta
                             start=(rhalf == 0),
                             stop=(rhalf == HALVES - 1),
                         )
+                contexts[g].append(o)
+                square_sum = work.tile([P, HALVES], F32, name="square_sum")
+                for half in range(HALVES):
+                    squares = work.tile([P, P + 1], BF16, name="squares", bufs=BLOCKS)
+                    nc.scalar.activation(out=squares[:], in_=o[:, half, :], func=ACT.Square, accum_out=square_sum[:, half : half + 1])
+                bits = square_sum[:].bitcast(U32)
+                guess_sq = work.tile([P, HALVES], F32, name="guess_sq")
+                nc.scalar.activation(out=guess_sq[:], in_=bits, func=ACT.Exp, scale=2.0 * LOG_STEP, bias=bias_guess_sq[:, 0:1])
+                log_guess = work.tile([P, HALVES], F32, name="log_guess")
+                nc.scalar.activation(out=log_guess[:], in_=bits, func=ACT.Identity, scale=LOG_STEP, bias=bias_log_guess[:, 0:1])
+                off_sq = work.tile([P, HALVES], F32, name="off_sq")
+                for half in range(HALVES):
+                    col = slice(half, half + 1)
+                    nc.scalar.activation(out=off_sq[:, col], in_=guess_sq[:, col], func=ACT.Square, scale=square_sum[:, col], bias=bias_fit[:, 0:1])
                 for half in range(HALVES):
                     block = word * HALVES + half
-                    squares = work.tile([P, P + 1], BF16, name="squares", bufs=BLOCKS)
-                    nc.scalar.activation(out=squares[:], in_=o[:, half, :], func=ACT.Square, accum_out=square_sum[:, block : block + 1])
-                contexts[g].append(o)
-            inv_norms[g] = work.tile([P, BLOCKS], F32, name="inv_norm", bufs=alive(CONTEXT, NORMALISE))
-            nc.gpsimd.tensor_tensor(out=inv_norms[g][:], in0=square_sum[:], in1=minus_half[:], op=ALU.pow)
+                    nc.scalar.activation(out=inv_norms[g][:, block : block + 1], in_=off_sq[:, half : half + 1], func=ACT.Exp, scale=FIT_A, bias=log_guess[:, half : half + 1])
 
         def normalise(g):
             normeds[g] = work.tile([P, BLOCKS, P], BF16, name="normed")

@@ -123,8 +123,11 @@ def tile_widthchartransformermlpheaderfastposv2_b_kernel(tc, x, pos, gamma, beta
                 nc.tensor.matmul(scores[g][:, block, :], lhsT=q16[g][:, block * P : (block + 1) * P, 1], rhs=k16[g][:, first : first + PLACES, 1], start=True, stop=True)
 
         def row_maxima(g):
-            tops[g] = work.tile([P, BLOCKS], BF16, name="top", bufs=alive(MAXIMA, WEIGHTS))
-            nc.vector.tensor_reduce(out=tops[g][:], in_=scores[g][:], axis=AXIS.X, op=ALU.max)
+            top32 = work.tile([P, BLOCKS], F32, name="top32", bufs=alive(MAXIMA, WEIGHTS))
+            for block in range(BLOCKS):
+                unused = work.tile([P, PLACES], BF16, name="unused", bufs=BLOCKS)
+                nc.vector.tensor_scalar(out=unused[:], in0=scores[g][:, block, :], scalar1=1.0, scalar2=None, op0=ALU.mult, op1=ALU.max, accum_out=top32[:, block : block + 1])
+            tops[g] = upper_halves(top32)
 
         def centre_values(g):
             vc_psum = psum.tile([P, BLOCKS, P], F32, name="vc_psum")
@@ -144,7 +147,7 @@ def tile_widthchartransformermlpheaderfastposv2_b_kernel(tc, x, pos, gamma, beta
                         block = word * HALVES + half
                         nc.tensor.matmul(
                             scores_t[:, rhalf, half * P : (half + 1) * P],
-                            lhsT=tops[g][:, block : block + 1].to_broadcast([P, P]),
+                            lhsT=tops[g][:, block : block + 1, 1].to_broadcast([P, P]),
                             rhs=minus_ident[:],
                             start=False,
                             stop=(half == HALVES - 1),
@@ -212,5 +215,5 @@ def tile_widthchartransformermlpheaderfastposv2_b_kernel(tc, x, pos, gamma, beta
             run(store, step - NORMALISE)
             run(centre_values, step - VALUES)
             run(score, step - SCORE)
-            run(look_up, step)
             run(row_maxima, step - MAXIMA)
+            run(look_up, step)

@@ -67,10 +67,10 @@ def tile_widthchartransformermlpheaderfastposv2_b_kernel(tc, x, pos, gamma, beta
         offsets = held.tile([P, WORDS * PLACES // 16], U16, name="offsets")
         nc.sync.dma_start(offsets[:], offs)
         pos2 = held.tile([P, PAIR], F32, name="pos2")
-        nc.scalar.dma_start(pos2[:, 0:PLACES], pos)
+        nc.sync.dma_start(pos2[:, 0:PLACES], pos)
         table = [held.tile([P, ALPHABET], F32, name="table%d" % c) for c in range(6)]
-        for c in (0, 2, 4, 1, 3, 5):
-            queue = nc.sync if c < 3 else nc.scalar
+        for n, c in enumerate((0, 2, 4, 1, 3, 5)):
+            queue = nc.sync if n % 3 == 2 else nc.scalar
             queue.dma_start(table[c][:], x_blocks[c])
         gamma_in = held.tile([P, 1], F32, name="gamma_in")
         nc.sync.dma_start(gamma_in[:], gamma)
@@ -100,6 +100,9 @@ def tile_widthchartransformermlpheaderfastposv2_b_kernel(tc, x, pos, gamma, beta
             nc.vector.memset(vc[:, :, P : P + 1], SUM_COL)
 
         q16, k16, v32, scores, tops, weights, contexts, inv_norms, normeds = {}, {}, {}, {}, {}, {}, {}, {}, {}
+
+        def look_ups_over(g, stage):
+            return g + stage >= GROUPS
 
         def upper_halves(tile32):
             return tile32[:].bitcast(BF16).rearrange("p (n two) -> p n two", two=2)
@@ -133,7 +136,10 @@ def tile_widthchartransformermlpheaderfastposv2_b_kernel(tc, x, pos, gamma, beta
             vc_psum = psum.tile([P, BLOCKS, P], F32, name="vc_psum")
             for block in range(BLOCKS):
                 nc.tensor.matmul(vc_psum[:, block, :], lhsT=v32[g][:, block * P : (block + 1) * P], rhs=centre[:], start=True, stop=True)
-            nc.scalar.copy(vc_ring[g % len(vc_ring)][:, :, 0:P], vc_psum[:])
+            if look_ups_over(g, VALUES):
+                nc.vector.tensor_copy(vc_ring[g % len(vc_ring)][:, :, 0:P], vc_psum[:])
+            else:
+                nc.scalar.copy(vc_ring[g % len(vc_ring)][:, :, 0:P], vc_psum[:])
 
         def attention_weights(g):
             weights[g] = []
@@ -193,7 +199,10 @@ def tile_widthchartransformermlpheaderfastposv2_b_kernel(tc, x, pos, gamma, beta
             normeds[g] = work.tile([P, BLOCKS, P], BF16, name="normed")
             for block in range(BLOCKS):
                 word, half = divmod(block, HALVES)
-                nc.scalar.activation(out=normeds[g][:, block, :], in_=contexts[g][word][:, half, 0:P], func=ACT.Copy, scale=inv_norms[g][:, block : block + 1])
+                if look_ups_over(g, NORMALISE):
+                    nc.vector.tensor_scalar(out=normeds[g][:, block, :], in0=contexts[g][word][:, half, 0:P], scalar1=inv_norms[g][:, block : block + 1], scalar2=None, op0=ALU.mult)
+                else:
+                    nc.scalar.activation(out=normeds[g][:, block, :], in_=contexts[g][word][:, half, 0:P], func=ACT.Copy, scale=inv_norms[g][:, block : block + 1])
 
         def store(g):
             pair, h = divmod(g, HEADS)
@@ -201,7 +210,10 @@ def tile_widthchartransformermlpheaderfastposv2_b_kernel(tc, x, pos, gamma, beta
             for block in range(BLOCKS):
                 nc.tensor.matmul(normed_psum[:, block * P : (block + 1) * P], lhsT=normeds[g][:, block, :], rhs=ident[:], start=True, stop=True)
             result = work.tile([P, PAIR], F32, name="result")
-            nc.scalar.activation(out=result[:], in_=normed_psum[:], func=ACT.Identity, scale=gamma_scaled[:, 0:1], bias=beta_in[:, 0:1])
+            if look_ups_over(g, NORMALISE):
+                nc.vector.tensor_scalar(out=result[:], in0=normed_psum[:], scalar1=gamma_scaled[:, 0:1], scalar2=beta_in[:, 0:1], op0=ALU.mult, op1=ALU.add)
+            else:
+                nc.scalar.activation(out=result[:], in_=normed_psum[:], func=ACT.Identity, scale=gamma_scaled[:, 0:1], bias=beta_in[:, 0:1])
             nc.sync.dma_start(out[h * P : (h + 1) * P, pair * PAIR : (pair + 1) * PAIR], result[:])
 
         def run(stage, g):
@@ -209,9 +221,9 @@ def tile_widthchartransformermlpheaderfastposv2_b_kernel(tc, x, pos, gamma, beta
                 stage(g)
 
         for step in range(GROUPS + NORMALISE):
+            run(attention_weights, step - WEIGHTS)
             run(normalise, step - NORMALISE)
             run(context, step - CONTEXT)
-            run(attention_weights, step - WEIGHTS)
             run(store, step - NORMALISE)
             run(centre_values, step - VALUES)
             run(score, step - SCORE)

@@ -19,6 +19,7 @@ WORDS = 32
 HALVES = PLACES // P
 PAIR = 2 * PLACES
 BLOCKS = PAIR // P
+QUARTER = PLACES // 4
 GROUPS = HEADS * WORDS // 2
 EPS = 1e-5
 SUM_COL = math.sqrt(P * EPS)
@@ -99,7 +100,7 @@ def tile_widthchartransformermlpheaderfastposv2_b_kernel(tc, x, pos, gamma, beta
         for vc in vc_ring:
             nc.vector.memset(vc[:, :, P : P + 1], SUM_COL)
 
-        q16, k16, v32, scores, tops, weights, contexts, inv_norms, normeds = {}, {}, {}, {}, {}, {}, {}, {}, {}
+        q16, k16, v32, scores, running, tops, weights, contexts, inv_norms, normeds = {}, {}, {}, {}, {}, {}, {}, {}, {}, {}
 
         def look_ups_over(g, stage):
             return g + stage >= GROUPS
@@ -107,17 +108,18 @@ def tile_widthchartransformermlpheaderfastposv2_b_kernel(tc, x, pos, gamma, beta
         def upper_halves(tile32):
             return tile32[:].bitcast(BF16).rearrange("p (n two) -> p n two", two=2)
 
-        def look_up(g):
+        def look_up(g, part):
             pair, h = divmod(g, HEADS)
             pair_offsets = offsets[:, pair * (PAIR // 16) : (pair + 1) * (PAIR // 16)]
-            q32 = work.tile([P, PAIR], F32, name="q32", bufs=alive(0, WEIGHTS))
-            nc.vector.tensor_tensor(q32[:], table[h][:].indirect(pair_offsets), pos2[:], ALU.add)
-            k32 = work.tile([P, PAIR], F32, name="k32", bufs=alive(0, WEIGHTS))
-            nc.vector.tensor_tensor(k32[:], table[2 + h][:].indirect(pair_offsets), pos2[:], ALU.add)
-            q16[g] = upper_halves(q32)
-            k16[g] = upper_halves(k32)
-            v32[g] = work.tile([P, PAIR], F32, name="v32", bufs=alive(0, VALUES))
-            nc.vector.tensor_tensor(v32[g][:], table[4 + h][:].indirect(pair_offsets), pos2[:], ALU.add)
+            bufs = alive(0, VALUES) if part == 2 else alive(0, WEIGHTS)
+            e32 = work.tile([P, PAIR], F32, name=("q32", "k32", "v32")[part], bufs=bufs)
+            nc.vector.tensor_tensor(e32[:], table[2 * part + h][:].indirect(pair_offsets), pos2[:], ALU.add)
+            if part == 0:
+                q16[g] = upper_halves(e32)
+            elif part == 1:
+                k16[g] = upper_halves(e32)
+            else:
+                v32[g] = e32
 
         def score(g):
             scores[g] = psum.tile([P, BLOCKS, PLACES], BF16, name="scores", bufs=alive(SCORE, MAXIMA))
@@ -125,12 +127,18 @@ def tile_widthchartransformermlpheaderfastposv2_b_kernel(tc, x, pos, gamma, beta
                 first = (block // HALVES) * PLACES
                 nc.tensor.matmul(scores[g][:, block, :], lhsT=q16[g][:, block * P : (block + 1) * P, 1], rhs=k16[g][:, first : first + PLACES, 1], start=True, stop=True)
 
+        def last_quarter(g):
+            running[g] = work.tile([P, BLOCKS, QUARTER], BF16, name="running_first")
+            nc.scalar.copy(running[g][:], scores[g][:, :, 3 * QUARTER : 4 * QUARTER])
+
+        def fold(g, quarter):
+            taken = work.tile([P, BLOCKS, QUARTER], BF16, name="running%d" % quarter)
+            nc.vector.tensor_tensor(taken[:], scores[g][:, :, quarter * QUARTER : (quarter + 1) * QUARTER], running[g][:], ALU.max)
+            running[g] = taken
+
         def row_maxima(g):
-            top32 = work.tile([P, BLOCKS], F32, name="top32", bufs=alive(MAXIMA, WEIGHTS))
-            for block in range(BLOCKS):
-                unused = work.tile([P, PLACES], BF16, name="unused", bufs=BLOCKS)
-                nc.vector.tensor_scalar(out=unused[:], in0=scores[g][:, block, :], scalar1=1.0, scalar2=None, op0=ALU.mult, op1=ALU.max, accum_out=top32[:, block : block + 1])
-            tops[g] = upper_halves(top32)
+            tops[g] = work.tile([P, BLOCKS], BF16, name="top")
+            nc.vector.tensor_reduce(out=tops[g][:], in_=running[g][:], axis=AXIS.X, op=ALU.max)
 
         def centre_values(g):
             vc_psum = psum.tile([P, BLOCKS, P], F32, name="vc_psum")
@@ -153,7 +161,7 @@ def tile_widthchartransformermlpheaderfastposv2_b_kernel(tc, x, pos, gamma, beta
                         block = word * HALVES + half
                         nc.tensor.matmul(
                             scores_t[:, rhalf, half * P : (half + 1) * P],
-                            lhsT=tops[g][:, block : block + 1, 1].to_broadcast([P, P]),
+                            lhsT=tops[g][:, block : block + 1].to_broadcast([P, P]),
                             rhs=minus_ident[:],
                             start=False,
                             stop=(half == HALVES - 1),
@@ -216,16 +224,19 @@ def tile_widthchartransformermlpheaderfastposv2_b_kernel(tc, x, pos, gamma, beta
                 nc.scalar.activation(out=result[:], in_=normed_psum[:], func=ACT.Identity, scale=gamma_scaled[:, 0:1], bias=beta_in[:, 0:1])
             nc.sync.dma_start(out[h * P : (h + 1) * P, pair * PAIR : (pair + 1) * PAIR], result[:])
 
-        def run(stage, g):
+        def run(stage, g, *part):
             if 0 <= g < GROUPS:
-                stage(g)
+                stage(g, *part)
 
         for step in range(GROUPS + NORMALISE):
+            run(score, step - SCORE)
             run(attention_weights, step - WEIGHTS)
             run(normalise, step - NORMALISE)
             run(context, step - CONTEXT)
+            run(last_quarter, step - SCORE)
             run(store, step - NORMALISE)
             run(centre_values, step - VALUES)
-            run(score, step - SCORE)
+            for part in range(3):
+                run(fold, step - MAXIMA, part)
+                run(look_up, step, part)
             run(row_maxima, step - MAXIMA)
-            run(look_up, step)

@@ -19,7 +19,6 @@ WORDS = 32
 HALVES = PLACES // P
 PAIR = 2 * PLACES
 BLOCKS = PAIR // P
-QUARTER = PLACES // 4
 GROUPS = HEADS * WORDS // 2
 EPS = 1e-5
 SUM_COL = math.sqrt(P * EPS)
@@ -100,7 +99,7 @@ def tile_widthchartransformermlpheaderfastposv2_b_kernel(tc, x, pos, gamma, beta
         for vc in vc_ring:
             nc.vector.memset(vc[:, :, P : P + 1], SUM_COL)
 
-        q16, k16, v32, scores, running, tops, weights, contexts, inv_norms, normeds = {}, {}, {}, {}, {}, {}, {}, {}, {}, {}
+        q16, k16, v32, scores, folded, tops, weights, contexts, inv_norms, normeds = {}, {}, {}, {}, {}, {}, {}, {}, {}, {}
 
         def look_ups_over(g, stage):
             return g + stage >= GROUPS
@@ -122,23 +121,27 @@ def tile_widthchartransformermlpheaderfastposv2_b_kernel(tc, x, pos, gamma, beta
                 v32[g] = e32
 
         def score(g):
-            scores[g] = psum.tile([P, BLOCKS, PLACES], BF16, name="scores", bufs=alive(SCORE, MAXIMA))
+            scores[g] = psum.tile([P, BLOCKS, PLACES], BF16, name="scores")
             for block in range(BLOCKS):
                 first = (block // HALVES) * PLACES
                 nc.tensor.matmul(scores[g][:, block, :], lhsT=q16[g][:, block * P : (block + 1) * P, 1], rhs=k16[g][:, first : first + PLACES, 1], start=True, stop=True)
 
-        def last_quarter(g):
-            running[g] = work.tile([P, BLOCKS, QUARTER], BF16, name="running_first")
-            nc.scalar.copy(running[g][:], scores[g][:, :, 3 * QUARTER : 4 * QUARTER])
+        def second_half(g):
+            folded[g] = work.tile([P, BLOCKS, PLACES // 2], BF16, name="second_half")
+            nc.scalar.copy(folded[g][:], scores[g][:, :, PLACES // 2 : PLACES])
 
-        def fold(g, quarter):
-            taken = work.tile([P, BLOCKS, QUARTER], BF16, name="running%d" % quarter)
-            nc.vector.tensor_tensor(taken[:], scores[g][:, :, quarter * QUARTER : (quarter + 1) * QUARTER], running[g][:], ALU.max)
-            running[g] = taken
+        def fold(g, n):
+            width = PLACES >> (n + 1)
+            halved = work.tile([P, BLOCKS, width], BF16, name="folded%d" % n)
+            if n == 0:
+                nc.vector.tensor_tensor(halved[:], scores[g][:, :, 0:width], folded[g][:], ALU.max)
+            else:
+                nc.vector.tensor_tensor(halved[:], folded[g][:, :, 0:width], folded[g][:, :, width : 2 * width], ALU.max)
+            folded[g] = halved
 
         def row_maxima(g):
             tops[g] = work.tile([P, BLOCKS], BF16, name="top")
-            nc.vector.tensor_reduce(out=tops[g][:], in_=running[g][:], axis=AXIS.X, op=ALU.max)
+            nc.vector.tensor_reduce(out=tops[g][:], in_=folded[g][:], axis=AXIS.X, op=ALU.max)
 
         def centre_values(g):
             vc_psum = psum.tile([P, BLOCKS, P], F32, name="vc_psum")
@@ -175,7 +178,7 @@ def tile_widthchartransformermlpheaderfastposv2_b_kernel(tc, x, pos, gamma, beta
             contexts[g] = []
             inv_norms[g] = work.tile([P, BLOCKS], F32, name="inv_norm", bufs=alive(CONTEXT, NORMALISE))
             for word in range(2):
-                o = psum.tile([P, HALVES, P + 1], F32, name="o", bufs=2)
+                o = psum.tile([P, HALVES, P + 1], F32, name="o", bufs=3)
                 for half in range(HALVES):
                     for rhalf in range(HALVES):
                         nc.tensor.matmul(
@@ -233,7 +236,7 @@ def tile_widthchartransformermlpheaderfastposv2_b_kernel(tc, x, pos, gamma, beta
             run(attention_weights, step - WEIGHTS)
             run(normalise, step - NORMALISE)
             run(context, step - CONTEXT)
-            run(last_quarter, step - SCORE)
+            run(second_half, step - SCORE)
             run(store, step - NORMALISE)
             run(centre_values, step - VALUES)
             for part in range(3):

@@ -19,6 +19,7 @@ WORDS = 32
 HALVES = PLACES // P
 PAIR = 2 * PLACES
 BLOCKS = PAIR // P
+QUARTER = PLACES // 4
 GROUPS = HEADS * WORDS // 2
 EPS = 1e-5
 SUM_COL = math.sqrt(P * EPS)
@@ -99,7 +100,7 @@ def tile_widthchartransformermlpheaderfastposv2_b_kernel(tc, x, pos, gamma, beta
         for vc in vc_ring:
             nc.vector.memset(vc[:, :, P : P + 1], SUM_COL)
 
-        q16, k16, v32, scores, folded, tops, weights, contexts, inv_norms, normeds = {}, {}, {}, {}, {}, {}, {}, {}, {}, {}
+        q16, k16, v32, scores, running, tops, weights, contexts, inv_norms, normeds = {}, {}, {}, {}, {}, {}, {}, {}, {}, {}
 
         def look_ups_over(g, stage):
             return g + stage >= GROUPS
@@ -121,27 +122,23 @@ def tile_widthchartransformermlpheaderfastposv2_b_kernel(tc, x, pos, gamma, beta
                 v32[g] = e32
 
         def score(g):
-            scores[g] = psum.tile([P, BLOCKS, PLACES], BF16, name="scores")
+            scores[g] = psum.tile([P, BLOCKS, PLACES], BF16, name="scores", bufs=alive(SCORE, MAXIMA))
             for block in range(BLOCKS):
                 first = (block // HALVES) * PLACES
                 nc.tensor.matmul(scores[g][:, block, :], lhsT=q16[g][:, block * P : (block + 1) * P, 1], rhs=k16[g][:, first : first + PLACES, 1], start=True, stop=True)
 
-        def second_half(g):
-            folded[g] = work.tile([P, BLOCKS, PLACES // 2], BF16, name="second_half")
-            nc.scalar.copy(folded[g][:], scores[g][:, :, PLACES // 2 : PLACES])
+        def last_quarter(g):
+            running[g] = work.tile([P, BLOCKS, QUARTER], BF16, name="running_first")
+            nc.scalar.copy(running[g][:], scores[g][:, :, 3 * QUARTER : 4 * QUARTER])
 
-        def fold(g, n):
-            width = PLACES >> (n + 1)
-            halved = work.tile([P, BLOCKS, width], BF16, name="folded%d" % n)
-            if n == 0:
-                nc.vector.tensor_tensor(halved[:], scores[g][:, :, 0:width], folded[g][:], ALU.max)
-            else:
-                nc.vector.tensor_tensor(halved[:], folded[g][:, :, 0:width], folded[g][:, :, width : 2 * width], ALU.max)
-            folded[g] = halved
+        def fold(g, quarter):
+            taken = work.tile([P, BLOCKS, QUARTER], BF16, name="running%d" % quarter)
+            nc.vector.tensor_tensor(taken[:], scores[g][:, :, quarter * QUARTER : (quarter + 1) * QUARTER], running[g][:], ALU.max)
+            running[g] = taken
 
         def row_maxima(g):
             tops[g] = work.tile([P, BLOCKS], BF16, name="top")
-            nc.vector.tensor_reduce(out=tops[g][:], in_=folded[g][:], axis=AXIS.X, op=ALU.max)
+            nc.vector.tensor_reduce(out=tops[g][:], in_=running[g][:], axis=AXIS.X, op=ALU.max)
 
         def centre_values(g):
             vc_psum = psum.tile([P, BLOCKS, P], F32, name="vc_psum")
@@ -178,7 +175,7 @@ def tile_widthchartransformermlpheaderfastposv2_b_kernel(tc, x, pos, gamma, beta
             contexts[g] = []
             inv_norms[g] = work.tile([P, BLOCKS], F32, name="inv_norm", bufs=alive(CONTEXT, NORMALISE))
             for word in range(2):
-                o = psum.tile([P, HALVES, P + 1], F32, name="o", bufs=3)
+                o = psum.tile([P, HALVES, P + 1], F32, name="o", bufs=2)
                 for half in range(HALVES):
                     for rhalf in range(HALVES):
                         nc.tensor.matmul(
@@ -188,11 +185,16 @@ def tile_widthchartransformermlpheaderfastposv2_b_kernel(tc, x, pos, gamma, beta
                             start=(rhalf == 0),
                             stop=(rhalf == HALVES - 1),
                         )
-                contexts[g].append(o)
                 square_sum = work.tile([P, HALVES], F32, name="square_sum")
                 for half in range(HALVES):
                     squares = work.tile([P, P + 1], BF16, name="squares", bufs=BLOCKS)
                     nc.scalar.activation(out=squares[:], in_=o[:, half, :], func=ACT.Square, accum_out=square_sum[:, half : half + 1])
+                if look_ups_over(g, CONTEXT):
+                    o_kept = work.tile([P, HALVES, P], F32, name="o_kept", bufs=2 * alive(CONTEXT, NORMALISE))
+                    nc.vector.tensor_copy(o_kept[:], o[:, :, 0:P])
+                    contexts[g].append(o_kept)
+                else:
+                    contexts[g].append(o)
                 bits = square_sum[:].bitcast(U32)
                 guess_sq = work.tile([P, HALVES], F32, name="guess_sq")
                 nc.scalar.activation(out=guess_sq[:], in_=bits, func=ACT.Exp, scale=2.0 * LOG_STEP, bias=bias_guess_sq[:, 0:1])
@@ -236,7 +238,7 @@ def tile_widthchartransformermlpheaderfastposv2_b_kernel(tc, x, pos, gamma, beta
             run(attention_weights, step - WEIGHTS)
             run(normalise, step - NORMALISE)
             run(context, step - CONTEXT)
-            run(second_half, step - SCORE)
+            run(last_quarter, step - SCORE)
             run(store, step - NORMALISE)
             run(centre_values, step - VALUES)
             for part in range(3):

@@ -236,12 +236,15 @@ def tile_widthchartransformermlpheaderfastposv2_b_kernel(tc, x, pos, gamma, beta
         for step in range(GROUPS + NORMALISE):
             run(score, step - SCORE)
             run(attention_weights, step - WEIGHTS)
+            run(last_quarter, step - SCORE)
             run(normalise, step - NORMALISE)
             run(context, step - CONTEXT)
-            run(last_quarter, step - SCORE)
             run(store, step - NORMALISE)
             run(centre_values, step - VALUES)
-            for part in range(3):
-                run(fold, step - MAXIMA, part)
-                run(look_up, step, part)
+            run(fold, step - MAXIMA, 1)
+            run(look_up, step, 0)
+            run(fold, step - MAXIMA, 2)
+            run(look_up, step, 1)
             run(row_maxima, step - MAXIMA)
+            run(fold, step - SCORE, 0)
+            run(look_up, step, 2)

@@ -94,6 +94,8 @@ def tile_widthchartransformermlpheaderfastposv2_b_kernel(tc, x, pos, gamma, beta
         nc.vector.memset(bias_log_guess[:], LOG_BASE + FIT_C)
         bias_fit = held.tile([P, 1], F32, name="bias_fit")
         nc.vector.memset(bias_fit[:], -FIT_T)
+        table_warm_up = held.tile([P, 1], F32, name="table_warm_up")
+        nc.scalar.activation(out=table_warm_up[:], in_=bias_fit[:], func=ACT.Exp)
         gamma_scaled = held.tile([P, 1], F32, name="gamma_scaled")
         nc.vector.tensor_scalar(out=gamma_scaled[:], in0=gamma_in[:], scalar1=math.sqrt(P), scalar2=None, op0=ALU.mult)
         vc_ring = [held.tile([P, BLOCKS, VC_STEP], BF16, name="vc%d" % n) for n in range(alive(VALUES, CONTEXT))]

@@ -45,7 +45,7 @@ MAXIMA = 2
 WEIGHTS = 3
 CONTEXT = 4
 NORMALISE = 5
-VALUES = CONTEXT // 2
+VALUES = 1
 
 
 def alive(written, last_read):

import math

import concourse.mybir as mybir
from concourse.masks import make_identity

F32 = mybir.dt.float32
BF16 = mybir.dt.bfloat16
U16 = mybir.dt.uint16
U32 = mybir.dt.uint32
ALU = mybir.AluOpType
ACT = mybir.ActivationFunctionType
AXIS = mybir.AxisListType

P = 128
HEADS = 2
ALPHABET = 512
PLACES = 256
WORDS = 32
HALVES = PLACES // P
PAIR = 2 * PLACES
BLOCKS = PAIR // P
QUARTER = PLACES // 4
GROUPS = HEADS * WORDS // 2
EPS = 1e-5
SUM_COL = math.sqrt(P * EPS)
VC_STEP = 136

LN2 = math.log(2.0)
M_PEAK = 1.0 / LN2 - 1.0
LOG_GAP = (math.log(1.0 + M_PEAK) / LN2 - M_PEAK) / 2.0
LOG_STEP = -(LN2 / 2.0) / 2.0**23
LOG_BASE = (LN2 / 2.0) * (127.0 - LOG_GAP)

FIT_HALF = 0.1
FIT_POINTS = [1.0 + FIT_HALF * math.cos((2 * n + 1) * math.pi / 6.0) for n in range(3)]
FIT_VALUES = [-0.5 * math.log(t) for t in FIT_POINTS]
SLOPE_01 = (FIT_VALUES[1] - FIT_VALUES[0]) / (FIT_POINTS[1] - FIT_POINTS[0])
SLOPE_12 = (FIT_VALUES[2] - FIT_VALUES[1]) / (FIT_POINTS[2] - FIT_POINTS[1])
FIT_A = (SLOPE_12 - SLOPE_01) / (FIT_POINTS[2] - FIT_POINTS[0])
FIT_T = (FIT_POINTS[0] + FIT_POINTS[1]) / 2.0 - SLOPE_01 / (2.0 * FIT_A)
FIT_C = FIT_VALUES[0] - FIT_A * (FIT_POINTS[0] - FIT_T) ** 2

SCORE = 1
MAXIMA = 2
WEIGHTS = 3
CONTEXT = 4
NORMALISE = 5
VALUES = 1


def alive(written, last_read):
    return last_read - written + 1


FLOPS = 2 * 2 * P * PLACES * PLACES * HEADS * WORDS


def tile_widthchartransformermlpheaderfastposv2_b_kernel(tc, x, pos, gamma, beta, offs, out):
    nc = tc.nc
    x_blocks = x.rearrange("(c p) s -> c p s", p=P)

    with (
        tc.tile_pool(name="held", bufs=1) as held,
        tc.tile_pool(name="work", bufs=2) as work,
        tc.psum_pool(name="psum", bufs=1) as psum,
        nc.allow_low_precision(reason="the row maximum is only a shift of the softmax"),
    ):
        offsets = held.tile([P, WORDS * PLACES // 16], U16, name="offsets")
        nc.sync.dma_start(offsets[:], offs)
        pos2 = held.tile([P, PAIR], F32, name="pos2")
        nc.sync.dma_start(pos2[:, 0:PLACES], pos)
        table = [held.tile([P, ALPHABET], F32, name="table%d" % c) for c in range(6)]
        for n, c in enumerate((0, 2, 4, 1, 3, 5)):
            queue = nc.sync if n % 3 == 2 else nc.scalar
            queue.dma_start(table[c][:], x_blocks[c])
        gamma_in = held.tile([P, 1], F32, name="gamma_in")
        nc.sync.dma_start(gamma_in[:], gamma)
        beta_in = held.tile([P, 1], F32, name="beta_in")
        nc.scalar.dma_start(beta_in[:], beta)

        nc.vector.tensor_copy(pos2[:, PLACES:PAIR], pos2[:, 0:PLACES])

        ident32 = held.tile([P, P], F32, name="ident32")
        make_identity(nc, ident32[:])
        centre = held.tile([P, P], F32, name="centre")
        nc.vector.tensor_scalar(out=centre[:], in0=ident32[:], scalar1=-1.0 / P, scalar2=None, op0=ALU.add)
        ident = held.tile([P, P], BF16, name="ident")
        make_identity(nc, ident[:])
        minus_ident = held.tile([P, P], BF16, name="minus_ident")
        nc.vector.tensor_scalar(out=minus_ident[:], in0=ident[:], scalar1=-1.0, scalar2=None, op0=ALU.mult)
        bias_guess_sq = held.tile([P, 1], F32, name="bias_guess_sq")
        nc.vector.memset(bias_guess_sq[:], 2.0 * LOG_BASE)
        bias_log_guess = held.tile([P, 1], F32, name="bias_log_guess")
        nc.vector.memset(bias_log_guess[:], LOG_BASE + FIT_C)
        bias_fit = held.tile([P, 1], F32, name="bias_fit")
        nc.vector.memset(bias_fit[:], -FIT_T)
        table_warm_up = held.tile([P, 1], F32, name="table_warm_up")
        nc.scalar.activation(out=table_warm_up[:], in_=bias_fit[:], func=ACT.Exp)
        gamma_scaled = held.tile([P, 1], F32, name="gamma_scaled")
        nc.vector.tensor_scalar(out=gamma_scaled[:], in0=gamma_in[:], scalar1=math.sqrt(P), scalar2=None, op0=ALU.mult)
        vc_ring = [held.tile([P, BLOCKS, VC_STEP], BF16, name="vc%d" % n) for n in range(alive(VALUES, CONTEXT))]
        for vc in vc_ring:
            nc.vector.memset(vc[:, :, P : P + 1], SUM_COL)

        q16, k16, v32, scores, running, tops, weights, contexts, inv_norms, normeds = {}, {}, {}, {}, {}, {}, {}, {}, {}, {}

        def look_ups_over(g, stage):
            return g + stage >= GROUPS

        def upper_halves(tile32):
            return tile32[:].bitcast(BF16).rearrange("p (n two) -> p n two", two=2)

        def look_up(g, part):
            pair, h = divmod(g, HEADS)
            pair_offsets = offsets[:, pair * (PAIR // 16) : (pair + 1) * (PAIR // 16)]
            bufs = alive(0, VALUES) if part == 2 else alive(0, WEIGHTS)
            e32 = work.tile([P, PAIR], F32, name=("q32", "k32", "v32")[part], bufs=bufs)
            nc.vector.tensor_tensor(e32[:], table[2 * part + h][:].indirect(pair_offsets), pos2[:], ALU.add)
            if part == 0:
                q16[g] = upper_halves(e32)
            elif part == 1:
                k16[g] = upper_halves(e32)
            else:
                v32[g] = e32

        def score(g):
            scores[g] = psum.tile([P, BLOCKS, PLACES], BF16, name="scores", bufs=alive(SCORE, MAXIMA))
            for block in range(BLOCKS):
                first = (block // HALVES) * PLACES
                nc.tensor.matmul(scores[g][:, block, :], lhsT=q16[g][:, block * P : (block + 1) * P, 1], rhs=k16[g][:, first : first + PLACES, 1], start=True, stop=True)

        def last_quarter(g):
            running[g] = work.tile([P, BLOCKS, QUARTER], BF16, name="running_first")
            nc.scalar.copy(running[g][:], scores[g][:, :, 3 * QUARTER : 4 * QUARTER])

        def fold(g, quarter):
            taken = work.tile([P, BLOCKS, QUARTER], BF16, name="running%d" % quarter)
            nc.vector.tensor_tensor(taken[:], scores[g][:, :, quarter * QUARTER : (quarter + 1) * QUARTER], running[g][:], ALU.max)
            running[g] = taken

        def row_maxima(g):
            tops[g] = work.tile([P, BLOCKS], BF16, name="top")
            nc.vector.tensor_reduce(out=tops[g][:], in_=running[g][:], axis=AXIS.X, op=ALU.max)

        def centre_values(g):
            vc_psum = psum.tile([P, BLOCKS, P], F32, name="vc_psum")
            for block in range(BLOCKS):
                nc.tensor.matmul(vc_psum[:, block, :], lhsT=v32[g][:, block * P : (block + 1) * P], rhs=centre[:], start=True, stop=True)
            if look_ups_over(g, VALUES):
                nc.vector.tensor_copy(vc_ring[g % len(vc_ring)][:, :, 0:P], vc_psum[:])
            else:
                nc.scalar.copy(vc_ring[g % len(vc_ring)][:, :, 0:P], vc_psum[:])

        def attention_weights(g):
            weights[g] = []
            for word in range(2):
                first = word * PLACES
                scores_t = psum.tile([P, HALVES, PLACES], F32, name="scores_t", bufs=2)
                for rhalf in range(HALVES):
                    r0 = first + rhalf * P
                    nc.tensor.matmul(scores_t[:, rhalf, :], lhsT=k16[g][:, r0 : r0 + P, 1], rhs=q16[g][:, first : first + PLACES, 1], start=True, stop=False)
                    for half in range(HALVES):
                        block = word * HALVES + half
                        nc.tensor.matmul(
                            scores_t[:, rhalf, half * P : (half + 1) * P],
                            lhsT=tops[g][:, block : block + 1].to_broadcast([P, P]),
                            rhs=minus_ident[:],
                            start=False,
                            stop=(half == HALVES - 1),
                        )
                w16 = work.tile([P, HALVES, PLACES], BF16, name="w16", bufs=2 * alive(WEIGHTS, CONTEXT))
                nc.scalar.activation(out=w16[:], in_=scores_t[:], func=ACT.Exp, scale=1.0 / math.sqrt(P))
                weights[g].append(w16)

        def context(g):
            vc = vc_ring[g % len(vc_ring)]
            contexts[g] = []
            inv_norms[g] = work.tile([P, BLOCKS], F32, name="inv_norm", bufs=alive(CONTEXT, NORMALISE))
            for word in range(2):
                o = psum.tile([P, HALVES, P + 1], F32, name="o", bufs=2)
                for half in range(HALVES):
                    for rhalf in range(HALVES):
                        nc.tensor.matmul(
                            o[:, half, :],
                            lhsT=weights[g][word][:, rhalf, half * P : (half + 1) * P],
                            rhs=vc[:, word * HALVES + rhalf, 0 : P + 1],
                            start=(rhalf == 0),
                            stop=(rhalf == HALVES - 1),
                        )
                square_sum = work.tile([P, HALVES], F32, name="square_sum")
                for half in range(HALVES):
                    squares = work.tile([P, P + 1], BF16, name="squares", bufs=BLOCKS)
                    nc.scalar.activation(out=squares[:], in_=o[:, half, :], func=ACT.Square, accum_out=square_sum[:, half : half + 1])
                if look_ups_over(g, CONTEXT):
                    o_kept = work.tile([P, HALVES, P], F32, name="o_kept", bufs=2 * alive(CONTEXT, NORMALISE))
                    nc.vector.tensor_copy(o_kept[:], o[:, :, 0:P])
                    contexts[g].append(o_kept)
                else:
                    contexts[g].append(o)
                bits = square_sum[:].bitcast(U32)
                guess_sq = work.tile([P, HALVES], F32, name="guess_sq")
                nc.scalar.activation(out=guess_sq[:], in_=bits, func=ACT.Exp, scale=2.0 * LOG_STEP, bias=bias_guess_sq[:, 0:1])
                log_guess = work.tile([P, HALVES], F32, name="log_guess")
                nc.scalar.activation(out=log_guess[:], in_=bits, func=ACT.Identity, scale=LOG_STEP, bias=bias_log_guess[:, 0:1])
                off_sq = work.tile([P, HALVES], F32, name="off_sq")
                for half in range(HALVES):
                    col = slice(half, half + 1)
                    nc.scalar.activation(out=off_sq[:, col], in_=guess_sq[:, col], func=ACT.Square, scale=square_sum[:, col], bias=bias_fit[:, 0:1])
                for half in range(HALVES):
                    block = word * HALVES + half
                    nc.scalar.activation(out=inv_norms[g][:, block : block + 1], in_=off_sq[:, half : half + 1], func=ACT.Exp, scale=FIT_A, bias=log_guess[:, half : half + 1])

        def normalise(g):
            normeds[g] = work.tile([P, BLOCKS, P], BF16, name="normed")
            for block in range(BLOCKS):
                word, half = divmod(block, HALVES)
                if look_ups_over(g, NORMALISE):
                    nc.vector.tensor_scalar(out=normeds[g][:, block, :], in0=contexts[g][word][:, half, 0:P], scalar1=inv_norms[g][:, block : block + 1], scalar2=None, op0=ALU.mult)
                else:
                    nc.scalar.activation(out=normeds[g][:, block, :], in_=contexts[g][word][:, half, 0:P], func=ACT.Copy, scale=inv_norms[g][:, block : block + 1])

        def store(g):
            pair, h = divmod(g, HEADS)
            normed_psum = psum.tile([P, PAIR], F32, name="normed_psum")
            for block in range(BLOCKS):
                nc.tensor.matmul(normed_psum[:, block * P : (block + 1) * P], lhsT=normeds[g][:, block, :], rhs=ident[:], start=True, stop=True)
            result = work.tile([P, PAIR], F32, name="result")
            if look_ups_over(g, NORMALISE):
                nc.vector.tensor_scalar(out=result[:], in0=normed_psum[:], scalar1=gamma_scaled[:, 0:1], scalar2=beta_in[:, 0:1], op0=ALU.mult, op1=ALU.add)
            else:
                nc.scalar.activation(out=result[:], in_=normed_psum[:], func=ACT.Identity, scale=gamma_scaled[:, 0:1], bias=beta_in[:, 0:1])
            nc.sync.dma_start(out[h * P : (h + 1) * P, pair * PAIR : (pair + 1) * PAIR], result[:])

        def run(stage, g, *part):
            if 0 <= g < GROUPS:
                stage(g, *part)

        for step in range(GROUPS + NORMALISE):
            run(score, step - SCORE)
            run(attention_weights, step - WEIGHTS)
            run(last_quarter, step - SCORE)
            run(normalise, step - NORMALISE)
            run(context, step - CONTEXT)
            run(store, step - NORMALISE)
            run(centre_values, step - VALUES)
            run(fold, step - MAXIMA, 1)
            run(look_up, step, 0)
            run(fold, step - MAXIMA, 2)
            run(look_up, step, 1)
            run(row_maxima, step - MAXIMA)
            run(fold, step - SCORE, 0)
            run(look_up, step, 2)
